import numpy as np
import ml_dtypes


def mxq(x, axis, fmt="e4m3"):
    dtype, down = {"e4m3": (ml_dtypes.float8_e4m3fn, 7), "e5m2": (ml_dtypes.float8_e5m2, 14)}[fmt]
    v = np.moveaxis(np.asarray(x, np.float32).astype(ml_dtypes.bfloat16).astype(np.float64), axis, -1)
    blocks = v.reshape(v.shape[:-1] + (-1, 32))
    amax = np.abs(blocks).max(-1, keepdims=True)
    byte = np.maximum(np.where(amax > 0, np.frexp(amax)[1] - 1 + 127, 0) - down, 1)
    scale = np.exp2(byte - 127.0)
    codes = (blocks / scale).astype(np.float32).astype(dtype).astype(np.float64)
    return np.moveaxis((codes * scale).reshape(v.shape), -1, axis)


WIDE = False


def mx_kscale(k):
    if not WIDE:
        return np.ones(k)
    levels = np.array([10, -10, 5, -5, 0])
    a = np.random.permutation(np.resize(levels, k // 512 * 4)).reshape(k // 512, 4)
    idx = np.arange(k)
    return np.exp2(a[idx // 512, idx % 128 // 32])


BF16 = ml_dtypes.bfloat16


def bf(x):
    return np.asarray(x, np.float32).astype(BF16)


def f64(x):
    return np.asarray(x).astype(np.float64)


B, D, F, R, HT, S = 4, 256, 512, 128, 1, 2048


def silu(v):
    return v / (1.0 + np.exp(-v))


def setup_inputs():
    t = mx_kscale(F)
    mlp = silu(np.random.standard_normal((B, F, HT, S))) * np.random.standard_normal((B, F, HT, S))
    return {
        "mlp": bf(mlp * t[None, :, None, None]),
        "down_snapped": bf(np.random.standard_normal((D, F)) * 1.5 / np.sqrt(F) / t[None, :]),
        "down_scale_A": bf(np.random.standard_normal((D, R))),
        "down_scale_B": bf(np.random.standard_normal((R, F)) / np.sqrt(R)),
    }


def reference(mlp, down_snapped, down_scale_A, down_scale_B):
    down_eff = f64(down_snapped) * (f64(down_scale_A) @ f64(down_scale_B))
    out = mxq(down_eff, 1, "e4m3") @ mxq(f64(mlp).reshape(B, F, HT * S), 1, "e4m3")
    return out.reshape(B, D, HT, S)

@@ -1,0 +1,165 @@
+from contextlib import ExitStack
+
+import concourse.mybir as mybir
+from concourse.masks import make_identity
+
+BF16 = mybir.dt.bfloat16
+F32 = mybir.dt.float32
+U32 = mybir.dt.uint32
+U8 = mybir.dt.uint8
+FP8X4 = mybir.dt.float8_e4m3fn_x4
+
+P = 128
+PACK = 4
+B, D, F, R, S = 4, 256, 512, 128, 2048
+MT = D // P
+UNIT = 1024
+NT = 512
+UPB = S // UNIT
+NUNITS = B * UPB
+SC = 192
+RUN = 4
+
+FLOPS = 2 * B * D * F * S + 2 * D * R * F
+
+
+def tile_ffnwithscales_pb_t_kernel(tc, mlp, down_snapped, down_scale_A, down_scale_B, out):
+    nc = tc.nc
+    with ExitStack() as ctx:
+        keep = ctx.enter_context(tc.tile_pool(name="keep", bufs=1))
+        ring = ctx.enter_context(tc.tile_pool(name="ring", bufs=3))
+        psum = ctx.enter_context(tc.psum_pool(name="psum", bufs=8))
+        ctx.enter_context(tc.manual_schedule())
+
+        a_sb = keep.tile([P, MT, R], BF16, name="a_sb")
+        nc.sync.dma_start(out=a_sb[:], in_=down_scale_A.rearrange("(p m) r -> p m r", m=MT))
+        b_sb = keep.tile([P, F], BF16, name="b_sb")
+        nc.sync.dma_start(out=b_sb[:], in_=down_scale_B)
+        snap = keep.tile([P, MT, F], BF16, name="snap")
+        nc.sync.dma_start(out=snap[:], in_=down_snapped.rearrange("(p m) c -> p m c", m=MT))
+        raw = []
+        for b in range(B):
+            raw_b = keep.tile([P, PACK, S], BF16, name="raw%d" % b)
+            raw.append(raw_b)
+            src = mlp[b].rearrange("(p j) h s -> p j (h s)", j=PACK)
+            if b == 0:
+                for h in range(UPB):
+                    cols = slice(h * UNIT, (h + 1) * UNIT)
+                    nc.sync.dma_start(out=raw_b[:, :, cols], in_=src[:, :, cols])
+            else:
+                nc.sync.dma_start(out=raw_b[:], in_=src)
+
+        res = []
+        for b in range(B):
+            res_b = keep.tile([P, MT, S], F32, name="res%d" % b)
+            res.append(res_b)
+
+        ident = keep.tile([P, P], BF16, name="ident")
+        make_identity(nc, ident[:])
+        at_ps = psum.tile([P, MT, P], BF16, name="at_ps", tag="bank")
+        for m in range(MT):
+            nc.tensor.transpose(at_ps[:, m, :], a_sb[:, m, :], ident[:])
+        at_sb = keep.tile([P, MT, P], BF16, name="at_sb")
+        nc.scalar.copy(out=at_sb[:], in_=at_ps[:])
+        eff = keep.tile([P, MT, PACK, P], BF16, name="eff")
+        for m in range(MT):
+            mult_ps = psum.tile([P, F], F32, name="mult_ps", tag="bank")
+            nc.tensor.matmul(out=mult_ps[:], lhsT=at_sb[:, m, :], rhs=b_sb[:], start=True, stop=True)
+            nc.vector.tensor_tensor(
+                out=eff[:, m],
+                in0=mult_ps[:].rearrange("p (q t) -> p t q", t=PACK),
+                in1=snap[:, m, :].rearrange("p (q t) -> p t q", t=PACK),
+                op=mybir.AluOpType.mult,
+            )
+        efft_ps = psum.tile([P, PACK, D], BF16, name="efft_ps", tag="bank")
+        for m in range(MT):
+            for t in range(PACK):
+                nc.tensor.transpose(efft_ps[:, t, m * P : (m + 1) * P], eff[:, m, t, :], ident[:])
+        w_grouped = keep.tile([P, D, PACK], BF16, name="w_grouped", align_bytes=64)
+        w_codes = keep.tile([P, D], U32, name="w_codes", align_bytes=64)
+        w_scales = keep.tile([P, D], U8, name="w_scales", align_bytes=64)
+
+        grouped = {}
+        codes = {}
+        scales = {}
+
+        def regroup(u):
+            b, h = divmod(u, UPB)
+            g = ring.tile([P, UNIT, PACK], BF16, name="grouped", align_bytes=64)
+            grouped[u] = g
+            c0 = h * UNIT
+            split = UNIT - SC
+            nc.vector.tensor_copy(
+                out=g[:, 0:split, :].rearrange("p (c i) t -> p c t i", i=RUN),
+                in_=raw[b][:, :, c0 : c0 + split].rearrange("p t (c i) -> p c t i", i=RUN),
+            )
+            nc.scalar.copy(
+                out=g[:, split:UNIT, :].rearrange("p (c i) t -> p c t i", i=RUN),
+                in_=raw[b][:, :, c0 + split : c0 + UNIT].rearrange("p t (c i) -> p c t i", i=RUN),
+            )
+
+        def quantise(u):
+            cd = ring.tile([P, UNIT], U32, name="codes", align_bytes=64)
+            sc = ring.tile([P, UNIT], U8, name="scales", align_bytes=64)
+            codes[u] = cd
+            scales[u] = sc
+            nc.vector.quantize_mx(
+                out=cd[:].bitcast(FP8X4),
+                scales=sc[:],
+                in_=grouped[u][:].rearrange("p w t -> p (w t)"),
+            )
+
+        def multiply(u):
+            accs = []
+            for m in range(MT):
+                for n in range(UNIT // NT):
+                    acc = psum.tile([P, NT], F32, name="acc", tag="bank")
+                    nc.tensor.matmul_mx(
+                        out=acc[:],
+                        lhsT=w_codes[:, m * P : (m + 1) * P].bitcast(FP8X4),
+                        lhsT_scale=w_scales[:, m * P : (m + 1) * P],
+                        rhs=codes[u][:, n * NT : (n + 1) * NT].bitcast(FP8X4),
+                        rhs_scale=scales[u][:, n * NT : (n + 1) * NT],
+                        start=True,
+                        stop=True,
+                    )
+                    accs.append((m, n, acc))
+            return accs
+
+        def drain(u, accs):
+            b, h = divmod(u, UPB)
+            for m, n, acc in accs:
+                c0 = h * UNIT + n * NT
+                dst = res[b][:, m, c0 : c0 + NT]
+                if u == NUNITS - 1 and m == 1:
+                    nc.vector.tensor_copy(out=dst, in_=acc[:])
+                else:
+                    nc.scalar.copy(out=dst, in_=acc[:])
+
+        def store(u):
+            b, h = divmod(u, UPB)
+            dst = out[b].rearrange("(p m) h s -> p m (h s)", m=MT)
+            if b < B - 1:
+                if h == UPB - 1:
+                    nc.sync.dma_start(out=dst, in_=res[b][:])
+            else:
+                cols = slice(h * UNIT, (h + 1) * UNIT)
+                nc.sync.dma_start(out=dst[:, :, cols], in_=res[b][:, :, cols])
+
+        regroup(0)
+        nc.scalar.copy(out=w_grouped[:], in_=efft_ps[:].rearrange("p t c -> p c t"))
+        regroup(1)
+        nc.vector.quantize_mx(
+            out=w_codes[:].bitcast(FP8X4),
+            scales=w_scales[:],
+            in_=w_grouped[:].rearrange("p c t -> p (c t)"),
+        )
+        quantise(0)
+        for u in range(NUNITS):
+            accs = multiply(u)
+            if u + 2 < NUNITS:
+                regroup(u + 2)
+            drain(u, accs)
+            if u + 1 < NUNITS:
+                quantise(u + 1)
+            store(u)

@@ -13,12 +13,17 @@ P = 128
 PACK = 4
 B, D, F, R, S = 4, 256, 512, 128, 2048
 MT = D // P
-UNIT = 1024
 NT = 512
-UPB = S // UNIT
-NUNITS = B * UPB
-SC = 192
 RUN = 4
+UNITS = [
+    (0, 0, 1024, 336, ()), (0, 1024, 1024, 336, ()),
+    (1, 0, 1024, 192, ()), (1, 1024, 1024, 192, ()),
+    (2, 0, 1024, 192, ()), (2, 1024, 1024, 192, ()),
+    (3, 0, 1024, 96, ()), (3, 1024, 512, 0, (1,)), (3, 1536, 512, 0, (1,)),
+]
+LOADS = [(0, 0, 1024), (0, 1024, 1024), (1, 0, 2048), (2, 0, 2048), (3, 0, 2048)]
+STORES = {1: [(0, 0, 2048)], 3: [(1, 0, 2048)], 4: [(2, 0, 1024)], 5: [(2, 1024, 1024)], 6: [(3, 0, 1024)], 7: [(3, 1024, 512)], 8: [(3, 1536, 512)]}
+RING = 4
 
 FLOPS = 2 * B * D * F * S + 2 * D * R * F
 
@@ -27,7 +32,7 @@ def tile_ffnwithscales_pb_t_kernel(tc, mlp, down_snapped, down_scale_A, down_sca
     nc = tc.nc
     with ExitStack() as ctx:
         keep = ctx.enter_context(tc.tile_pool(name="keep", bufs=1))
-        ring = ctx.enter_context(tc.tile_pool(name="ring", bufs=3))
+        ring = ctx.enter_context(tc.tile_pool(name="ring", bufs=RING))
         psum = ctx.enter_context(tc.psum_pool(name="psum", bufs=8))
         ctx.enter_context(tc.manual_schedule())
 
@@ -38,21 +43,18 @@ def tile_ffnwithscales_pb_t_kernel(tc, mlp, down_snapped, down_scale_A, down_sca
         snap = keep.tile([P, MT, F], BF16, name="snap")
         nc.sync.dma_start(out=snap[:], in_=down_snapped.rearrange("(p m) c -> p m c", m=MT))
         raw = []
+        res = []
         for b in range(B):
             raw_b = keep.tile([P, PACK, S], BF16, name="raw%d" % b)
             raw.append(raw_b)
-            src = mlp[b].rearrange("(p j) h s -> p j (h s)", j=PACK)
-            if b == 0:
-                for h in range(UPB):
-                    cols = slice(h * UNIT, (h + 1) * UNIT)
-                    nc.sync.dma_start(out=raw_b[:, :, cols], in_=src[:, :, cols])
-            else:
-                nc.sync.dma_start(out=raw_b[:], in_=src)
-
-        res = []
-        for b in range(B):
             res_b = keep.tile([P, MT, S], F32, name="res%d" % b)
             res.append(res_b)
+        for b, c0, w in LOADS:
+            src = mlp[b].rearrange("(p j) h s -> p j (h s)", j=PACK)
+            if w == S:
+                nc.sync.dma_start(out=raw[b][:], in_=src)
+            else:
+                nc.sync.dma_start(out=raw[b][:, :, c0 : c0 + w], in_=src[:, :, c0 : c0 + w])
 
         ident = keep.tile([P, P], BF16, name="ident")
         make_identity(nc, ident[:])
@@ -82,70 +84,72 @@ def tile_ffnwithscales_pb_t_kernel(tc, mlp, down_snapped, down_scale_A, down_sca
         grouped = {}
         codes = {}
         scales = {}
+        WMAX = max(u[2] for u in UNITS)
 
-        def regroup(u):
-            b, h = divmod(u, UPB)
-            g = ring.tile([P, UNIT, PACK], BF16, name="grouped", align_bytes=64)
-            grouped[u] = g
-            c0 = h * UNIT
-            split = UNIT - SC
+        def regroup(i):
+            b, c0, w, sc, vd = UNITS[i]
+            g = ring.tile([P, WMAX, PACK], BF16, name="grouped", align_bytes=64)
+            grouped[i] = g
+            split = w - sc
             nc.vector.tensor_copy(
                 out=g[:, 0:split, :].rearrange("p (c i) t -> p c t i", i=RUN),
                 in_=raw[b][:, :, c0 : c0 + split].rearrange("p t (c i) -> p c t i", i=RUN),
             )
-            nc.scalar.copy(
-                out=g[:, split:UNIT, :].rearrange("p (c i) t -> p c t i", i=RUN),
-                in_=raw[b][:, :, c0 + split : c0 + UNIT].rearrange("p t (c i) -> p c t i", i=RUN),
-            )
+            if sc > 0:
+                nc.scalar.copy(
+                    out=g[:, split:w, :].rearrange("p (c i) t -> p c t i", i=RUN),
+                    in_=raw[b][:, :, c0 + split : c0 + w].rearrange("p t (c i) -> p c t i", i=RUN),
+                )
 
-        def quantise(u):
-            cd = ring.tile([P, UNIT], U32, name="codes", align_bytes=64)
-            sc = ring.tile([P, UNIT], U8, name="scales", align_bytes=64)
-            codes[u] = cd
-            scales[u] = sc
+        def quantise(i):
+            w = UNITS[i][2]
+            cd = ring.tile([P, WMAX], U32, name="codes", align_bytes=64)
+            sc = ring.tile([P, WMAX], U8, name="scales", align_bytes=64)
+            codes[i] = cd
+            scales[i] = sc
             nc.vector.quantize_mx(
-                out=cd[:].bitcast(FP8X4),
-                scales=sc[:],
-                in_=grouped[u][:].rearrange("p w t -> p (w t)"),
+                out=cd[:, 0:w].bitcast(FP8X4),
+                scales=sc[:, 0:w],
+                in_=grouped[i][:, 0:w, :].rearrange("p w t -> p (w t)"),
             )
 
-        def multiply(u):
+        def multiply(i):
+            w = UNITS[i][2]
+            nt = min(w, NT)
             accs = []
-            for m in range(MT):
-                for n in range(UNIT // NT):
+            for n in range(w // nt):
+                for m in range(MT):
                     acc = psum.tile([P, NT], F32, name="acc", tag="bank")
                     nc.tensor.matmul_mx(
-                        out=acc[:],
+                        out=acc[:, 0:nt],
                         lhsT=w_codes[:, m * P : (m + 1) * P].bitcast(FP8X4),
                         lhsT_scale=w_scales[:, m * P : (m + 1) * P],
-                        rhs=codes[u][:, n * NT : (n + 1) * NT].bitcast(FP8X4),
-                        rhs_scale=scales[u][:, n * NT : (n + 1) * NT],
+                        rhs=codes[i][:, n * nt : (n + 1) * nt].bitcast(FP8X4),
+                        rhs_scale=scales[i][:, n * nt : (n + 1) * nt],
                         start=True,
                         stop=True,
                     )
-                    accs.append((m, n, acc))
+                    accs.append((m, n, nt, acc))
             return accs
 
-        def drain(u, accs):
-            b, h = divmod(u, UPB)
-            for m, n, acc in accs:
-                c0 = h * UNIT + n * NT
-                dst = res[b][:, m, c0 : c0 + NT]
-                if u == NUNITS - 1 and m == 1:
-                    nc.vector.tensor_copy(out=dst, in_=acc[:])
-                else:
-                    nc.scalar.copy(out=dst, in_=acc[:])
+        def drain(i, accs, on_vector):
+            b, c0, w, sc, vd = UNITS[i]
+            for k, (m, n, nt, acc) in enumerate(accs):
+                dst = res[b][:, m, c0 + n * nt : c0 + (n + 1) * nt]
+                if k in vd and on_vector:
+                    nc.vector.tensor_copy(out=dst, in_=acc[:, 0:nt])
+                if k not in vd and not on_vector:
+                    nc.scalar.copy(out=dst, in_=acc[:, 0:nt])
 
-        def store(u):
-            b, h = divmod(u, UPB)
-            dst = out[b].rearrange("(p m) h s -> p m (h s)", m=MT)
-            if b < B - 1:
-                if h == UPB - 1:
+        def store(i):
+            for b, c0, w in STORES.get(i, []):
+                dst = out[b].rearrange("(p m) h s -> p m (h s)", m=MT)
+                if w == S:
                     nc.sync.dma_start(out=dst, in_=res[b][:])
-            else:
-                cols = slice(h * UNIT, (h + 1) * UNIT)
-                nc.sync.dma_start(out=dst[:, :, cols], in_=res[b][:, :, cols])
+                else:
+                    nc.sync.dma_start(out=dst[:, :, c0 : c0 + w], in_=res[b][:, :, c0 : c0 + w])
 
+        n_units = len(UNITS)
         regroup(0)
         nc.scalar.copy(out=w_grouped[:], in_=efft_ps[:].rearrange("p t c -> p c t"))
         regroup(1)
@@ -155,11 +159,13 @@ def tile_ffnwithscales_pb_t_kernel(tc, mlp, down_snapped, down_scale_A, down_sca
             in_=w_grouped[:].rearrange("p c t -> p (c t)"),
         )
         quantise(0)
-        for u in range(NUNITS):
-            accs = multiply(u)
-            if u + 2 < NUNITS:
-                regroup(u + 2)
-            drain(u, accs)
-            if u + 1 < NUNITS:
-                quantise(u + 1)
-            store(u)
+        quantise(1)
+        for i in range(n_units):
+            accs = multiply(i)
+            drain(i, accs, False)
+            if i + 2 < n_units:
+                regroup(i + 2)
+            if 1 <= i and i + 1 < n_units:
+                quantise(i + 1)
+            drain(i, accs, True)
+            store(i)

@@ -19,10 +19,10 @@ UNITS = [
     (0, 0, 1024, 336, ()), (0, 1024, 1024, 336, ()),
     (1, 0, 1024, 192, ()), (1, 1024, 1024, 192, ()),
     (2, 0, 1024, 192, ()), (2, 1024, 1024, 192, ()),
-    (3, 0, 1024, 96, ()), (3, 1024, 512, 0, (1,)), (3, 1536, 512, 0, (1,)),
+    (3, 0, 1024, 96, ()), (3, 1024, 512, 0, (1,)), (3, 1536, 256, 0, (1,)), (3, 1792, 256, 0, (1,)),
 ]
 LOADS = [(0, 0, 1024), (0, 1024, 1024), (1, 0, 2048), (2, 0, 2048), (3, 0, 2048)]
-STORES = {1: [(0, 0, 2048)], 3: [(1, 0, 2048)], 4: [(2, 0, 1024)], 5: [(2, 1024, 1024)], 6: [(3, 0, 1024)], 7: [(3, 1024, 512)], 8: [(3, 1536, 512)]}
+STORES = {1: [(0, 0, 2048)], 3: [(1, 0, 2048)], 4: [(2, 0, 1024)], 5: [(2, 1024, 1024)], 6: [(3, 0, 1024)], 7: [(3, 1024, 512)], 8: [(3, 1536, 256)], 9: [(3, 1792, 256)]}
 RING = 4
 
 FLOPS = 2 * B * D * F * S + 2 * D * R * F

@@ -17,12 +17,12 @@ NT = 512
 RUN = 4
 UNITS = [
     (0, 0, 1024, 336, ()), (0, 1024, 1024, 336, ()),
-    (1, 0, 1024, 192, ()), (1, 1024, 1024, 192, ()),
+    (1, 0, 1024, 320, ()), (1, 1024, 1024, 224, ()),
     (2, 0, 1024, 192, ()), (2, 1024, 1024, 192, ()),
-    (3, 0, 1024, 96, ()), (3, 1024, 512, 0, (1,)), (3, 1536, 256, 0, (1,)), (3, 1792, 256, 0, (1,)),
+    (3, 0, 1024, 96, ()), (3, 1024, 512, 0, (1,)), (3, 1536, 512, 0, (1,)),
 ]
 LOADS = [(0, 0, 1024), (0, 1024, 1024), (1, 0, 2048), (2, 0, 2048), (3, 0, 2048)]
-STORES = {1: [(0, 0, 2048)], 3: [(1, 0, 2048)], 4: [(2, 0, 1024)], 5: [(2, 1024, 1024)], 6: [(3, 0, 1024)], 7: [(3, 1024, 512)], 8: [(3, 1536, 256)], 9: [(3, 1792, 256)]}
+STORES = {1: [(0, 0, 2048)], 2: [(1, 0, 1024)], 3: [(1, 1024, 1024)], 4: [(2, 0, 1024)], 5: [(2, 1024, 1024)], 6: [(3, 0, 1024)], 7: [(3, 1024, 512)], 8: [(3, 1536, 512)]}
 RING = 4
 
 FLOPS = 2 * B * D * F * S + 2 * D * R * F
@@ -152,13 +152,13 @@ def tile_ffnwithscales_pb_t_kernel(tc, mlp, down_snapped, down_scale_A, down_sca
         n_units = len(UNITS)
         regroup(0)
         nc.scalar.copy(out=w_grouped[:], in_=efft_ps[:].rearrange("p t c -> p c t"))
-        regroup(1)
+        quantise(0)
         nc.vector.quantize_mx(
             out=w_codes[:].bitcast(FP8X4),
             scales=w_scales[:],
             in_=w_grouped[:].rearrange("p c t -> p (c t)"),
         )
-        quantise(0)
+        regroup(1)
         quantise(1)
         for i in range(n_units):
             accs = multiply(i)

@@ -42,19 +42,20 @@ def tile_ffnwithscales_pb_t_kernel(tc, mlp, down_snapped, down_scale_A, down_sca
         nc.sync.dma_start(out=b_sb[:], in_=down_scale_B)
         snap = keep.tile([P, MT, F], BF16, name="snap")
         nc.sync.dma_start(out=snap[:], in_=down_snapped.rearrange("(p m) c -> p m c", m=MT))
-        raw = []
+        raw = {}
         res = []
         for b in range(B):
-            raw_b = keep.tile([P, PACK, S], BF16, name="raw%d" % b)
-            raw.append(raw_b)
             res_b = keep.tile([P, MT, S], F32, name="res%d" % b)
             res.append(res_b)
         for b, c0, w in LOADS:
             src = mlp[b].rearrange("(p j) h s -> p j (h s)", j=PACK)
+            piece = keep.tile([P, PACK, w], BF16, name="raw%d_%d" % (b, c0))
+            for c in range(c0, c0 + w, 256):
+                raw[(b, c)] = (piece, c0)
             if w == S:
-                nc.sync.dma_start(out=raw[b][:], in_=src)
+                nc.sync.dma_start(out=piece[:], in_=src)
             else:
-                nc.sync.dma_start(out=raw[b][:, :, c0 : c0 + w], in_=src[:, :, c0 : c0 + w])
+                nc.sync.dma_start(out=piece[:], in_=src[:, :, c0 : c0 + w])
 
         ident = keep.tile([P, P], BF16, name="ident")
         make_identity(nc, ident[:])
@@ -91,14 +92,16 @@ def tile_ffnwithscales_pb_t_kernel(tc, mlp, down_snapped, down_scale_A, down_sca
             g = ring.tile([P, WMAX, PACK], BF16, name="grouped", align_bytes=64)
             grouped[i] = g
             split = w - sc
+            piece, base = raw[(b, c0)]
+            c0 = c0 - base
             nc.vector.tensor_copy(
                 out=g[:, 0:split, :].rearrange("p (c i) t -> p c t i", i=RUN),
-                in_=raw[b][:, :, c0 : c0 + split].rearrange("p t (c i) -> p c t i", i=RUN),
+                in_=piece[:, :, c0 : c0 + split].rearrange("p t (c i) -> p c t i", i=RUN),
             )
             if sc > 0:
                 nc.scalar.copy(
                     out=g[:, split:w, :].rearrange("p (c i) t -> p c t i", i=RUN),
-                    in_=raw[b][:, :, c0 + split : c0 + w].rearrange("p t (c i) -> p c t i", i=RUN),
+                    in_=piece[:, :, c0 + split : c0 + w].rearrange("p t (c i) -> p c t i", i=RUN),
                 )
 
         def quantise(i):

@@ -36,20 +36,20 @@ def tile_ffnwithscales_pb_t_kernel(tc, mlp, down_snapped, down_scale_A, down_sca
         psum = ctx.enter_context(tc.psum_pool(name="psum", bufs=8))
         ctx.enter_context(tc.manual_schedule())
 
-        a_sb = keep.tile([P, MT, R], BF16, name="a_sb")
+        a_sb = keep.tile([P, MT, R], BF16, name="a_sb", align_bytes=512)
         nc.sync.dma_start(out=a_sb[:], in_=down_scale_A.rearrange("(p m) r -> p m r", m=MT))
-        b_sb = keep.tile([P, F], BF16, name="b_sb")
+        b_sb = keep.tile([P, F], BF16, name="b_sb", align_bytes=512)
         nc.sync.dma_start(out=b_sb[:], in_=down_scale_B)
-        snap = keep.tile([P, MT, F], BF16, name="snap")
+        snap = keep.tile([P, MT, F], BF16, name="snap", align_bytes=512)
         nc.sync.dma_start(out=snap[:], in_=down_snapped.rearrange("(p m) c -> p m c", m=MT))
         raw = {}
         res = []
         for b in range(B):
-            res_b = keep.tile([P, MT, S], F32, name="res%d" % b)
+            res_b = keep.tile([P, MT, S], F32, name="res%d" % b, align_bytes=4096)
             res.append(res_b)
         for b, c0, w in LOADS:
             src = mlp[b].rearrange("(p j) h s -> p j (h s)", j=PACK)
-            piece = keep.tile([P, PACK, w], BF16, name="raw%d_%d" % (b, c0))
+            piece = keep.tile([P, PACK, w], BF16, name="raw%d_%d" % (b, c0), align_bytes=4096)
             for c in range(c0, c0 + w, 256):
                 raw[(b, c)] = (piece, c0)
             if w == S:

@@ -22,7 +22,7 @@ UNITS = [
     (3, 0, 1024, 96, ()), (3, 1024, 512, 0, (1,)), (3, 1536, 512, 0, (1,)),
 ]
 LOADS = [(0, 0, 1024), (0, 1024, 1024), (1, 0, 2048), (2, 0, 2048), (3, 0, 2048)]
-STORES = {1: [(0, 0, 2048)], 2: [(1, 0, 1024)], 3: [(1, 1024, 1024)], 4: [(2, 0, 1024)], 5: [(2, 1024, 1024)], 6: [(3, 0, 1024)], 7: [(3, 1024, 512)], 8: [(3, 1536, 512)]}
+STORES = {1: [(0, 0, 2048)], 3: [(1, 0, 2048)], 4: [(2, 0, 1024)], 5: [(2, 1024, 1024)], 6: [(3, 0, 1024)], 8: [(3, 1024, 1024)]}
 RING = 4
 
 FLOPS = 2 * B * D * F * S + 2 * D * R * F

@@ -36,20 +36,20 @@ def tile_ffnwithscales_pb_t_kernel(tc, mlp, down_snapped, down_scale_A, down_sca
         psum = ctx.enter_context(tc.psum_pool(name="psum", bufs=8))
         ctx.enter_context(tc.manual_schedule())
 
-        a_sb = keep.tile([P, MT, R], BF16, name="a_sb", align_bytes=512)
+        a_sb = keep.tile([P, MT, R], BF16, name="a_sb", align_bytes=256)
         nc.sync.dma_start(out=a_sb[:], in_=down_scale_A.rearrange("(p m) r -> p m r", m=MT))
-        b_sb = keep.tile([P, F], BF16, name="b_sb", align_bytes=512)
+        b_sb = keep.tile([P, F], BF16, name="b_sb", align_bytes=256)
         nc.sync.dma_start(out=b_sb[:], in_=down_scale_B)
-        snap = keep.tile([P, MT, F], BF16, name="snap", align_bytes=512)
+        snap = keep.tile([P, MT, F], BF16, name="snap", align_bytes=256)
         nc.sync.dma_start(out=snap[:], in_=down_snapped.rearrange("(p m) c -> p m c", m=MT))
         raw = {}
         res = []
         for b in range(B):
-            res_b = keep.tile([P, MT, S], F32, name="res%d" % b, align_bytes=4096)
+            res_b = keep.tile([P, MT, S], F32, name="res%d" % b, align_bytes=256)
             res.append(res_b)
         for b, c0, w in LOADS:
             src = mlp[b].rearrange("(p j) h s -> p j (h s)", j=PACK)
-            piece = keep.tile([P, PACK, w], BF16, name="raw%d_%d" % (b, c0), align_bytes=4096)
+            piece = keep.tile([P, PACK, w], BF16, name="raw%d_%d" % (b, c0), align_bytes=256)
             for c in range(c0, c0 + w, 256):
                 raw[(b, c)] = (piece, c0)
             if w == S:

@@ -45,7 +45,7 @@ def tile_ffnwithscales_pb_t_kernel(tc, mlp, down_snapped, down_scale_A, down_sca
         raw = {}
         res = []
         for b in range(B):
-            res_b = keep.tile([P, MT, S], F32, name="res%d" % b, align_bytes=256)
+            res_b = keep.tile([P, MT, S], F32, name="res%d" % b)
             res.append(res_b)
         for b, c0, w in LOADS:
             src = mlp[b].rearrange("(p j) h s -> p j (h s)", j=PACK)

@@ -42,6 +42,8 @@ def tile_ffnwithscales_pb_t_kernel(tc, mlp, down_snapped, down_scale_A, down_sca
         nc.sync.dma_start(out=b_sb[:], in_=down_scale_B)
         snap = keep.tile([P, MT, F], BF16, name="snap", align_bytes=256)
         nc.sync.dma_start(out=snap[:], in_=down_snapped.rearrange("(p m) c -> p m c", m=MT))
+        pad = keep.tile([P, 16], BF16, name="pad")
+        nc.gpsimd.memset(pad[:], 0.0)
         raw = {}
         res = []
         for b in range(B):

@@ -83,6 +83,11 @@ def tile_ffnwithscales_pb_t_kernel(tc, mlp, down_snapped, down_scale_A, down_sca
         w_grouped = keep.tile([P, D, PACK], BF16, name="w_grouped", align_bytes=64)
         w_codes = keep.tile([P, D], U32, name="w_codes", align_bytes=64)
         w_scales = keep.tile([P, D], U8, name="w_scales", align_bytes=64)
+        w_half = []
+        for h in range(2):
+            w_half_h = keep.tile([P, D], U32, name="w_half%d" % h, align_bytes=64)
+            nc.gpsimd.memset(w_half_h[:], 0)
+            w_half.append(w_half_h)
 
         grouped = {}
         codes = {}
@@ -125,15 +130,16 @@ def tile_ffnwithscales_pb_t_kernel(tc, mlp, down_snapped, down_scale_A, down_sca
             for n in range(w // nt):
                 for m in range(MT):
                     acc = psum.tile([P, NT], F32, name="acc", tag="bank")
-                    nc.tensor.matmul_mx(
-                        out=acc[:, 0:nt],
-                        lhsT=w_codes[:, m * P : (m + 1) * P].bitcast(FP8X4),
-                        lhsT_scale=w_scales[:, m * P : (m + 1) * P],
-                        rhs=codes[i][:, n * nt : (n + 1) * nt].bitcast(FP8X4),
-                        rhs_scale=scales[i][:, n * nt : (n + 1) * nt],
-                        start=True,
-                        stop=True,
-                    )
+                    for h in range(2):
+                        nc.tensor.matmul_mx(
+                            out=acc[:, 0:nt],
+                            lhsT=w_half[h][:, m * P : (m + 1) * P].bitcast(FP8X4),
+                            lhsT_scale=w_scales[:, m * P : (m + 1) * P],
+                            rhs=codes[i][:, n * nt : (n + 1) * nt].bitcast(FP8X4),
+                            rhs_scale=scales[i][:, n * nt : (n + 1) * nt],
+                            start=(h == 0),
+                            stop=(h == 1),
+                        )
                     accs.append((m, n, nt, acc))
             return accs
 
@@ -163,6 +169,11 @@ def tile_ffnwithscales_pb_t_kernel(tc, mlp, down_snapped, down_scale_A, down_sca
             scales=w_scales[:],
             in_=w_grouped[:].rearrange("p c t -> p (c t)"),
         )
+        for h in range(2):
+            nc.vector.tensor_copy(
+                out=w_half[h][:].bitcast(U8).rearrange("p (c t) -> p c t", t=PACK)[:, :, 2 * h : 2 * h + 2],
+                in_=w_codes[:].bitcast(U8).rearrange("p (c t) -> p c t", t=PACK)[:, :, 2 * h : 2 * h + 2],
+            )
         regroup(1)
         quantise(1)
         for i in range(n_units):

@@ -16,13 +16,19 @@ MT = D // P
 NT = 512
 RUN = 4
 UNITS = [
-    (0, 0, 1024, 336, ()), (0, 1024, 1024, 336, ()),
-    (1, 0, 1024, 320, ()), (1, 1024, 1024, 224, ()),
-    (2, 0, 1024, 192, ()), (2, 1024, 1024, 192, ()),
-    (3, 0, 1024, 96, ()), (3, 1024, 512, 0, (1,)), (3, 1536, 512, 0, (1,)),
+    (0, 0, 512, 192, ()),
+    (0, 512, 512, 192, ()),
+    (0, 1024, 1024, 384, ()),
+    (1, 0, 1024, 320, ()),
+    (1, 1024, 1024, 256, ()),
+    (2, 0, 1024, 208, ()),
+    (2, 1024, 1024, 208, ()),
+    (3, 0, 1024, 128, ()),
+    (3, 1024, 512, 0, (1,)),
+    (3, 1536, 512, 0, (1,)),
 ]
-LOADS = [(0, 0, 1024), (0, 1024, 1024), (1, 0, 2048), (2, 0, 2048), (3, 0, 2048)]
-STORES = {1: [(0, 0, 2048)], 3: [(1, 0, 2048)], 4: [(2, 0, 1024)], 5: [(2, 1024, 1024)], 6: [(3, 0, 1024)], 8: [(3, 1024, 1024)]}
+LOADS = [(0, 0, 1024), (0, 1024, 1024), (1, 0, 1024), (1, 1024, 1024), (2, 0, 2048), (3, 0, 2048)]
+STORES = {2: [(0, 0, 2048)], 3: [(1, 0, 1024)], 4: [(1, 1024, 1024)], 5: [(2, 0, 1024)], 6: [(2, 1024, 1024)], 7: [(3, 0, 1024)], 9: [(3, 1024, 1024)]}
 RING = 4
 
 FLOPS = 2 * B * D * F * S + 2 * D * R * F
@@ -38,12 +44,10 @@ def tile_ffnwithscales_pb_t_kernel(tc, mlp, down_snapped, down_scale_A, down_sca
 
         a_sb = keep.tile([P, MT, R], BF16, name="a_sb", align_bytes=256)
         nc.sync.dma_start(out=a_sb[:], in_=down_scale_A.rearrange("(p m) r -> p m r", m=MT))
-        b_sb = keep.tile([P, F], BF16, name="b_sb", align_bytes=256)
-        nc.sync.dma_start(out=b_sb[:], in_=down_scale_B)
         snap = keep.tile([P, MT, F], BF16, name="snap", align_bytes=256)
         nc.sync.dma_start(out=snap[:], in_=down_snapped.rearrange("(p m) c -> p m c", m=MT))
-        pad = keep.tile([P, 16], BF16, name="pad")
-        nc.gpsimd.memset(pad[:], 0.0)
+        b_sb = keep.tile([P, F], BF16, name="b_sb", align_bytes=256)
+        nc.sync.dma_start(out=b_sb[:], in_=down_scale_B)
         raw = {}
         res = []
         for b in range(B):
@@ -66,21 +70,30 @@ def tile_ffnwithscales_pb_t_kernel(tc, mlp, down_snapped, down_scale_A, down_sca
             nc.tensor.transpose(at_ps[:, m, :], a_sb[:, m, :], ident[:])
         at_sb = keep.tile([P, MT, P], BF16, name="at_sb")
         nc.scalar.copy(out=at_sb[:], in_=at_ps[:])
-        eff = keep.tile([P, MT, PACK, P], BF16, name="eff")
+        snap_t = keep.tile([P, MT, PACK, P], BF16, name="snap_t")
+        snap_by_t = snap[:].rearrange("p m (q t) -> p m t q", t=PACK)
+        b_by_t = b_sb[:].rearrange("p (q t) -> p t q", t=PACK)
         for m in range(MT):
-            mult_ps = psum.tile([P, F], F32, name="mult_ps", tag="bank")
-            nc.tensor.matmul(out=mult_ps[:], lhsT=at_sb[:, m, :], rhs=b_sb[:], start=True, stop=True)
+            snap_ps = psum.tile([P, PACK, P], BF16, name="snap_ps", tag="bank")
+            for t in range(PACK):
+                nc.tensor.transpose(snap_ps[:, t, :], snap_by_t[:, m, t, :], ident[:])
+            if m == 0:
+                nc.scalar.copy(out=snap_t[:, m], in_=snap_ps[:])
+            else:
+                nc.vector.tensor_copy(out=snap_t[:, m], in_=snap_ps[:])
+        w_grouped = keep.tile([P, D, PACK], BF16, name="w_grouped", align_bytes=64)
+        for m in range(MT):
+            mult_ps = psum.tile([P, PACK, P], F32, name="mult_ps", tag="bank")
+            for t in range(PACK):
+                nc.tensor.matmul(
+                    out=mult_ps[:, t, :], lhsT=b_by_t[:, t, :], rhs=at_sb[:, m, :], start=True, stop=True
+                )
             nc.vector.tensor_tensor(
-                out=eff[:, m],
-                in0=mult_ps[:].rearrange("p (q t) -> p t q", t=PACK),
-                in1=snap[:, m, :].rearrange("p (q t) -> p t q", t=PACK),
+                out=w_grouped[:, m * P : (m + 1) * P, :],
+                in0=mult_ps[:].rearrange("p t o -> p o t"),
+                in1=snap_t[:, m].rearrange("p t o -> p o t"),
                 op=mybir.AluOpType.mult,
             )
-        efft_ps = psum.tile([P, PACK, D], BF16, name="efft_ps", tag="bank")
-        for m in range(MT):
-            for t in range(PACK):
-                nc.tensor.transpose(efft_ps[:, t, m * P : (m + 1) * P], eff[:, m, t, :], ident[:])
-        w_grouped = keep.tile([P, D, PACK], BF16, name="w_grouped", align_bytes=64)
         w_codes = keep.tile([P, D], U32, name="w_codes", align_bytes=64)
         w_scales = keep.tile([P, D], U8, name="w_scales", align_bytes=64)
         w_half = []
@@ -94,18 +107,21 @@ def tile_ffnwithscales_pb_t_kernel(tc, mlp, down_snapped, down_scale_A, down_sca
         scales = {}
         WMAX = max(u[2] for u in UNITS)
 
-        def regroup(i):
+        def regroup(i, on_vector):
             b, c0, w, sc, vd = UNITS[i]
-            g = ring.tile([P, WMAX, PACK], BF16, name="grouped", align_bytes=64)
-            grouped[i] = g
+            if i not in grouped:
+                g = ring.tile([P, WMAX, PACK], BF16, name="grouped", align_bytes=64)
+                grouped[i] = g
+            g = grouped[i]
             split = w - sc
             piece, base = raw[(b, c0)]
             c0 = c0 - base
-            nc.vector.tensor_copy(
-                out=g[:, 0:split, :].rearrange("p (c i) t -> p c t i", i=RUN),
+            if on_vector:
+                nc.vector.tensor_copy(
+                    out=g[:, 0:split, :].rearrange("p (c i) t -> p c t i", i=RUN),
                 in_=piece[:, :, c0 : c0 + split].rearrange("p t (c i) -> p c t i", i=RUN),
             )
-            if sc > 0:
+            if sc > 0 and not on_vector:
                 nc.scalar.copy(
                     out=g[:, split:w, :].rearrange("p (c i) t -> p c t i", i=RUN),
                     in_=piece[:, :, c0 + split : c0 + w].rearrange("p t (c i) -> p c t i", i=RUN),
@@ -161,27 +177,32 @@ def tile_ffnwithscales_pb_t_kernel(tc, mlp, down_snapped, down_scale_A, down_sca
                     nc.sync.dma_start(out=dst[:, :, c0 : c0 + w], in_=res[b][:, :, c0 : c0 + w])
 
         n_units = len(UNITS)
-        regroup(0)
-        nc.scalar.copy(out=w_grouped[:], in_=efft_ps[:].rearrange("p t c -> p c t"))
-        quantise(0)
+        regroup(0, False)
+        regroup(0, True)
         nc.vector.quantize_mx(
             out=w_codes[:].bitcast(FP8X4),
             scales=w_scales[:],
             in_=w_grouped[:].rearrange("p c t -> p (c t)"),
         )
+        quantise(0)
         for h in range(2):
             nc.vector.tensor_copy(
                 out=w_half[h][:].bitcast(U8).rearrange("p (c t) -> p c t", t=PACK)[:, :, 2 * h : 2 * h + 2],
                 in_=w_codes[:].bitcast(U8).rearrange("p (c t) -> p c t", t=PACK)[:, :, 2 * h : 2 * h + 2],
             )
-        regroup(1)
+        regroup(1, False)
+        regroup(1, True)
         quantise(1)
         for i in range(n_units):
             accs = multiply(i)
-            drain(i, accs, False)
             if i + 2 < n_units:
-                regroup(i + 2)
-            if 1 <= i and i + 1 < n_units:
+                regroup(i + 2, False)
+            drain(i, accs, False)
+            if i + 3 >= n_units and i + 1 < n_units:
+                quantise(i + 1)
+            if i + 2 < n_units:
+                regroup(i + 2, True)
+            if 1 <= i and i + 3 < n_units:
                 quantise(i + 1)
             drain(i, accs, True)
             store(i)

@@ -94,12 +94,15 @@ def tile_ffnwithscales_pb_t_kernel(tc, mlp, down_snapped, down_scale_A, down_sca
                 in1=snap_t[:, m].rearrange("p t o -> p o t"),
                 op=mybir.AluOpType.mult,
             )
-        w_codes = keep.tile([P, D], U32, name="w_codes", align_bytes=64)
+        w_words = keep.tile([P, 3, D], U32, name="w_words", align_bytes=64)
+        nc.gpsimd.memset(w_words[:, 0, :], 0)
+        nc.gpsimd.memset(w_words[:, 2, :], 0)
+        w_codes = w_words[:, 1, :]
+        w_bytes = w_words[:].bitcast(U8).rearrange("p s (c t) -> p c s t", t=PACK)
         w_scales = keep.tile([P, D], U8, name="w_scales", align_bytes=64)
         w_half = []
         for h in range(2):
             w_half_h = keep.tile([P, D], U32, name="w_half%d" % h, align_bytes=64)
-            nc.gpsimd.memset(w_half_h[:], 0)
             w_half.append(w_half_h)
 
         grouped = {}
@@ -180,15 +183,15 @@ def tile_ffnwithscales_pb_t_kernel(tc, mlp, down_snapped, down_scale_A, down_sca
         regroup(0, False)
         regroup(0, True)
         nc.vector.quantize_mx(
-            out=w_codes[:].bitcast(FP8X4),
+            out=w_codes.bitcast(FP8X4),
             scales=w_scales[:],
             in_=w_grouped[:].rearrange("p c t -> p (c t)"),
         )
         quantise(0)
         for h in range(2):
             nc.vector.tensor_copy(
-                out=w_half[h][:].bitcast(U8).rearrange("p (c t) -> p c t", t=PACK)[:, :, 2 * h : 2 * h + 2],
-                in_=w_codes[:].bitcast(U8).rearrange("p (c t) -> p c t", t=PACK)[:, :, 2 * h : 2 * h + 2],
+                out=w_half[h][:].bitcast(U8).rearrange("p (c s t) -> p c s t", s=2, t=2),
+                in_=w_bytes[:, :, 1 - h : 3 - h, 2 * h : 2 * h + 2],
             )
         regroup(1, False)
         regroup(1, True)

from contextlib import ExitStack

import concourse.mybir as mybir
from concourse.masks import make_identity

BF16 = mybir.dt.bfloat16
F32 = mybir.dt.float32
U32 = mybir.dt.uint32
U8 = mybir.dt.uint8
FP8X4 = mybir.dt.float8_e4m3fn_x4

P = 128
PACK = 4
B, D, F, R, S = 4, 256, 512, 128, 2048
MT = D // P
NT = 512
RUN = 4
UNITS = [
    (0, 0, 512, 192, ()),
    (0, 512, 512, 192, ()),
    (0, 1024, 1024, 384, ()),
    (1, 0, 1024, 320, ()),
    (1, 1024, 1024, 256, ()),
    (2, 0, 1024, 208, ()),
    (2, 1024, 1024, 208, ()),
    (3, 0, 1024, 128, ()),
    (3, 1024, 512, 0, (1,)),
    (3, 1536, 512, 0, (1,)),
]
LOADS = [(0, 0, 1024), (0, 1024, 1024), (1, 0, 1024), (1, 1024, 1024), (2, 0, 2048), (3, 0, 2048)]
STORES = {2: [(0, 0, 2048)], 3: [(1, 0, 1024)], 4: [(1, 1024, 1024)], 5: [(2, 0, 1024)], 6: [(2, 1024, 1024)], 7: [(3, 0, 1024)], 9: [(3, 1024, 1024)]}
RING = 4

FLOPS = 2 * B * D * F * S + 2 * D * R * F


def tile_ffnwithscales_pb_t_kernel(tc, mlp, down_snapped, down_scale_A, down_scale_B, out):
    nc = tc.nc
    with ExitStack() as ctx:
        keep = ctx.enter_context(tc.tile_pool(name="keep", bufs=1))
        ring = ctx.enter_context(tc.tile_pool(name="ring", bufs=RING))
        psum = ctx.enter_context(tc.psum_pool(name="psum", bufs=8))
        ctx.enter_context(tc.manual_schedule())

        a_sb = keep.tile([P, MT, R], BF16, name="a_sb", align_bytes=256)
        nc.sync.dma_start(out=a_sb[:], in_=down_scale_A.rearrange("(p m) r -> p m r", m=MT))
        snap = keep.tile([P, MT, F], BF16, name="snap", align_bytes=256)
        nc.sync.dma_start(out=snap[:], in_=down_snapped.rearrange("(p m) c -> p m c", m=MT))
        b_sb = keep.tile([P, F], BF16, name="b_sb", align_bytes=256)
        nc.sync.dma_start(out=b_sb[:], in_=down_scale_B)
        raw = {}
        res = []
        for b in range(B):
            res_b = keep.tile([P, MT, S], F32, name="res%d" % b)
            res.append(res_b)
        for b, c0, w in LOADS:
            src = mlp[b].rearrange("(p j) h s -> p j (h s)", j=PACK)
            piece = keep.tile([P, PACK, w], BF16, name="raw%d_%d" % (b, c0), align_bytes=256)
            for c in range(c0, c0 + w, 256):
                raw[(b, c)] = (piece, c0)
            if w == S:
                nc.sync.dma_start(out=piece[:], in_=src)
            else:
                nc.sync.dma_start(out=piece[:], in_=src[:, :, c0 : c0 + w])

        ident = keep.tile([P, P], BF16, name="ident")
        make_identity(nc, ident[:])
        at_ps = psum.tile([P, MT, P], BF16, name="at_ps", tag="bank")
        for m in range(MT):
            nc.tensor.transpose(at_ps[:, m, :], a_sb[:, m, :], ident[:])
        at_sb = keep.tile([P, MT, P], BF16, name="at_sb")
        nc.scalar.copy(out=at_sb[:], in_=at_ps[:])
        snap_t = keep.tile([P, MT, PACK, P], BF16, name="snap_t")
        snap_by_t = snap[:].rearrange("p m (q t) -> p m t q", t=PACK)
        b_by_t = b_sb[:].rearrange("p (q t) -> p t q", t=PACK)
        for m in range(MT):
            snap_ps = psum.tile([P, PACK, P], BF16, name="snap_ps", tag="bank")
            for t in range(PACK):
                nc.tensor.transpose(snap_ps[:, t, :], snap_by_t[:, m, t, :], ident[:])
            if m == 0:
                nc.scalar.copy(out=snap_t[:, m], in_=snap_ps[:])
            else:
                nc.vector.tensor_copy(out=snap_t[:, m], in_=snap_ps[:])
        w_grouped = keep.tile([P, D, PACK], BF16, name="w_grouped", align_bytes=64)
        for m in range(MT):
            mult_ps = psum.tile([P, PACK, P], F32, name="mult_ps", tag="bank")
            for t in range(PACK):
                nc.tensor.matmul(
                    out=mult_ps[:, t, :], lhsT=b_by_t[:, t, :], rhs=at_sb[:, m, :], start=True, stop=True
                )
            nc.vector.tensor_tensor(
                out=w_grouped[:, m * P : (m + 1) * P, :],
                in0=mult_ps[:].rearrange("p t o -> p o t"),
                in1=snap_t[:, m].rearrange("p t o -> p o t"),
                op=mybir.AluOpType.mult,
            )
        w_words = keep.tile([P, 3, D], U32, name="w_words", align_bytes=64)
        nc.gpsimd.memset(w_words[:, 0, :], 0)
        nc.gpsimd.memset(w_words[:, 2, :], 0)
        w_codes = w_words[:, 1, :]
        w_bytes = w_words[:].bitcast(U8).rearrange("p s (c t) -> p c s t", t=PACK)
        w_scales = keep.tile([P, D], U8, name="w_scales", align_bytes=64)
        w_half = []
        for h in range(2):
            w_half_h = keep.tile([P, D], U32, name="w_half%d" % h, align_bytes=64)
            w_half.append(w_half_h)

        grouped = {}
        codes = {}
        scales = {}
        WMAX = max(u[2] for u in UNITS)

        def regroup(i, on_vector):
            b, c0, w, sc, vd = UNITS[i]
            if i not in grouped:
                g = ring.tile([P, WMAX, PACK], BF16, name="grouped", align_bytes=64)
                grouped[i] = g
            g = grouped[i]
            split = w - sc
            piece, base = raw[(b, c0)]
            c0 = c0 - base
            if on_vector:
                nc.vector.tensor_copy(
                    out=g[:, 0:split, :].rearrange("p (c i) t -> p c t i", i=RUN),
                in_=piece[:, :, c0 : c0 + split].rearrange("p t (c i) -> p c t i", i=RUN),
            )
            if sc > 0 and not on_vector:
                nc.scalar.copy(
                    out=g[:, split:w, :].rearrange("p (c i) t -> p c t i", i=RUN),
                    in_=piece[:, :, c0 + split : c0 + w].rearrange("p t (c i) -> p c t i", i=RUN),
                )

        def quantise(i):
            w = UNITS[i][2]
            cd = ring.tile([P, WMAX], U32, name="codes", align_bytes=64)
            sc = ring.tile([P, WMAX], U8, name="scales", align_bytes=64)
            codes[i] = cd
            scales[i] = sc
            nc.vector.quantize_mx(
                out=cd[:, 0:w].bitcast(FP8X4),
                scales=sc[:, 0:w],
                in_=grouped[i][:, 0:w, :].rearrange("p w t -> p (w t)"),
            )

        def multiply(i):
            w = UNITS[i][2]
            nt = min(w, NT)
            accs = []
            for n in range(w // nt):
                for m in range(MT):
                    acc = psum.tile([P, NT], F32, name="acc", tag="bank")
                    for h in range(2):
                        nc.tensor.matmul_mx(
                            out=acc[:, 0:nt],
                            lhsT=w_half[h][:, m * P : (m + 1) * P].bitcast(FP8X4),
                            lhsT_scale=w_scales[:, m * P : (m + 1) * P],
                            rhs=codes[i][:, n * nt : (n + 1) * nt].bitcast(FP8X4),
                            rhs_scale=scales[i][:, n * nt : (n + 1) * nt],
                            start=(h == 0),
                            stop=(h == 1),
                        )
                    accs.append((m, n, nt, acc))
            return accs

        def drain(i, accs, on_vector):
            b, c0, w, sc, vd = UNITS[i]
            for k, (m, n, nt, acc) in enumerate(accs):
                dst = res[b][:, m, c0 + n * nt : c0 + (n + 1) * nt]
                if k in vd and on_vector:
                    nc.vector.tensor_copy(out=dst, in_=acc[:, 0:nt])
                if k not in vd and not on_vector:
                    nc.scalar.copy(out=dst, in_=acc[:, 0:nt])

        def store(i):
            for b, c0, w in STORES.get(i, []):
                dst = out[b].rearrange("(p m) h s -> p m (h s)", m=MT)
                if w == S:
                    nc.sync.dma_start(out=dst, in_=res[b][:])
                else:
                    nc.sync.dma_start(out=dst[:, :, c0 : c0 + w], in_=res[b][:, :, c0 : c0 + w])

        n_units = len(UNITS)
        regroup(0, False)
        regroup(0, True)
        nc.vector.quantize_mx(
            out=w_codes.bitcast(FP8X4),
            scales=w_scales[:],
            in_=w_grouped[:].rearrange("p c t -> p (c t)"),
        )
        quantise(0)
        for h in range(2):
            nc.vector.tensor_copy(
                out=w_half[h][:].bitcast(U8).rearrange("p (c s t) -> p c s t", s=2, t=2),
                in_=w_bytes[:, :, 1 - h : 3 - h, 2 * h : 2 * h + 2],
            )
        regroup(1, False)
        regroup(1, True)
        quantise(1)
        for i in range(n_units):
            accs = multiply(i)
            if i + 2 < n_units:
                regroup(i + 2, False)
            drain(i, accs, False)
            if i + 3 >= n_units and i + 1 < n_units:
                quantise(i + 1)
            if i + 2 < n_units:
                regroup(i + 2, True)
            if 1 <= i and i + 3 < n_units:
                quantise(i + 1)
            drain(i, accs, True)
            store(i)
